import numpy as np
import ml_dtypes


def mxq(x, axis, fmt="e4m3"):
    dtype, down = {"e4m3": (ml_dtypes.float8_e4m3fn, 7), "e5m2": (ml_dtypes.float8_e5m2, 14)}[fmt]
    v = np.moveaxis(np.asarray(x, np.float32).astype(ml_dtypes.bfloat16).astype(np.float64), axis, -1)
    blocks = v.reshape(v.shape[:-1] + (-1, 32))
    amax = np.abs(blocks).max(-1, keepdims=True)
    byte = np.maximum(np.where(amax > 0, np.frexp(amax)[1] - 1 + 127, 0) - down, 1)
    scale = np.exp2(byte - 127.0)
    codes = (blocks / scale).astype(np.float32).astype(dtype).astype(np.float64)
    return np.moveaxis((codes * scale).reshape(v.shape), -1, axis)


WIDE = False


def mx_kscale(k):
    if not WIDE:
        return np.ones(k)
    levels = np.array([10, -10, 5, -5, 0])
    a = np.random.permutation(np.resize(levels, k // 512 * 4)).reshape(k // 512, 4)
    idx = np.arange(k)
    return np.exp2(a[idx // 512, idx % 128 // 32])


BF16 = ml_dtypes.bfloat16


def bf(x):
    return np.asarray(x, np.float32).astype(BF16)


def f64(x):
    return np.asarray(x).astype(np.float64)


B, N, D, LAYER_NUM = 4, 2048, 512, 2


def setup_inputs():
    fin = mx_kscale(D)
    user = bf(np.random.standard_normal((B, N, D)) * fin)
    parts = []
    for l in range(LAYER_NUM):
        fout = mx_kscale(D) if l + 1 < LAYER_NUM else np.ones(D)
        parts.append((np.random.standard_normal((B, D, D)) * 1.2 / np.sqrt(D) / fin[:, None] * fout).reshape(B, D * D))
        parts.append(np.random.standard_normal((B, D)) * 0.5 * fout)
        fin = fout
    return {"user_emb": user, "item_emb": bf(np.concatenate(parts, axis=1))}


def reference(user_emb, item_emb):
    x = f64(user_emb)
    item = f64(item_emb)
    nb = x.shape[0]
    off = 0
    for _ in range(LAYER_NUM):
        W = item[:, off:off + D * D].reshape(nb, D, D)
        off += D * D
        b = item[:, off:off + D].reshape(nb, 1, D)
        off += D
        x = np.maximum((mxq(x, 2, "e4m3") @ mxq(W, 1, "e4m3")) + b, 0.0)
    return x

@@ -1,0 +1,268 @@
+from contextlib import ExitStack
+
+import concourse.mybir as mybir
+from concourse.masks import make_identity
+
+F32 = mybir.dt.float32
+BF16 = mybir.dt.bfloat16
+U32 = mybir.dt.uint32
+U8 = mybir.dt.uint8
+FP8X4 = mybir.dt.float8_e4m3fn_x4
+ACT = mybir.ActivationFunctionType
+ALU = mybir.AluOpType
+
+PINNED = False
+
+P = 128
+NB = 4
+NTOK = 2048
+D = 512
+PACK = 4
+TILES = 4
+CHUNK = TILES * P
+NCH = NTOK // CHUNK
+APP = NTOK // P
+TOTAL = NB * NCH
+OFF_W = (0, D * D + D)
+OFF_B0 = D * D
+OFF_B1 = 2 * D * D + D
+FLT_MAX = 3.4028234663852886e38
+
+FLOPS = 2 * NB * NTOK * D * D * 2
+
+
+def tile_can_t_kernel(tc, user_emb, item_emb, out):
+    nc = tc.nc
+    with ExitStack() as ctx:
+        if PINNED:
+            ctx.enter_context(tc.manual_schedule())
+        const = ctx.enter_context(tc.tile_pool(name="const", bufs=1))
+        wstage = ctx.enter_context(tc.tile_pool(name="wstage", bufs=2))
+        xq = ctx.enter_context(tc.tile_pool(name="xq", bufs=2))
+        hstage = ctx.enter_context(tc.tile_pool(name="hstage", bufs=2))
+        hq = ctx.enter_context(tc.tile_pool(name="hq", bufs=2))
+        ostage = ctx.enter_context(tc.tile_pool(name="ostage", bufs=4))
+        ps_t = ctx.enter_context(tc.psum_pool(name="ps_t", bufs=2))
+        ps_h = ctx.enter_context(tc.psum_pool(name="ps_h", bufs=4))
+        ps_o = ctx.enter_context(tc.psum_pool(name="ps_o", bufs=2))
+
+        ones = const.tile([P, P], BF16, name="ones")
+        nc.vector.memset(ones[:], 1.0)
+        b0rows = const.tile([P, D], BF16, name="b0rows")
+        nc.vector.memset(b0rows[:], 0.0)
+        b1row = const.tile([P, NB * D], BF16, name="b1row")
+        nc.vector.memset(b1row[:], 0.0)
+        nc.scalar.dma_start(out=b0rows[0:NB, :], in_=item_emb[:, OFF_B0 : OFF_B0 + D])
+        nc.scalar.dma_start(
+            out=b1row[0:1, :].rearrange("o (b e) -> o b e", b=NB),
+            in_=item_emb[:, OFF_B1 : OFF_B1 + D].unsqueeze(0),
+        )
+        ident_f = const.tile([P, P], F32, name="ident_f")
+        make_identity(nc, ident_f[:])
+        ident_b = const.tile([P, P], BF16, name="ident_b")
+        make_identity(nc, ident_b[:])
+
+        wraw = {}
+        xraw = {}
+
+        def load_w(b, layer):
+            t = const.tile([P, PACK, D], BF16, name="wraw%d%d" % (b, layer))
+            flat = item_emb[b, OFF_W[layer] : OFF_W[layer] + D * D]
+            if layer == 0:
+                nc.sync.dma_start(
+                    out=t[:].rearrange("p (u e) c -> p u (e c)", u=2),
+                    in_=flat.rearrange("(u p f) -> p u f", u=2, p=P, f=2 * D),
+                )
+            else:
+                nc.sync.dma_start(out=t[:], in_=flat.rearrange("(t p c) -> p t c", t=PACK, p=P, c=D))
+            wraw[(b, layer)] = t
+
+        def load_x(i):
+            b, c = divmod(i, NCH)
+            t = const.tile([P, TILES, D], BF16, name="xraw%d" % i)
+            src = user_emb[b].rearrange("(p a) k -> p a k", a=APP)
+            nc.sync.dma_start(out=t[:], in_=src[:, TILES * c : TILES * (c + 1), :])
+            xraw[i] = t
+
+        load_w(0, 0)
+        load_x(0)
+        load_w(0, 1)
+        for i in range(1, 5):
+            load_x(i)
+        load_w(1, 0)
+        load_w(1, 1)
+        for i in range(5, 8):
+            load_x(i)
+
+        wcodes = const.tile([P, 2 * NB, D], U32, name="wcodes", align_bytes=64)
+        wscales = const.tile([P, 2 * NB, D], U8, name="wscales", align_bytes=64)
+        wgrp = {}
+        HALF = D // 4 // 2
+
+        def regroup_w(b, layer, part):
+            if part is None or part == 0:
+                wgrp[(b, layer)] = wstage.tile([P, D, PACK], BF16, name="wgrp", tag="wgrp", align_bytes=64)
+            dst = wgrp[(b, layer)][:].rearrange("p (c i) t -> p c t i", i=4)
+            src = wraw[(b, layer)][:].rearrange("p t (c i) -> p c t i", i=4)
+            if part is None:
+                nc.vector.tensor_copy(out=dst, in_=src)
+            else:
+                cols = slice(HALF * part, HALF * (part + 1))
+                nc.scalar.copy(out=dst[:, cols, :, :], in_=src[:, cols, :, :])
+
+        def quant_w(b, layer):
+            j = 2 * b + layer
+            nc.vector.quantize_mx(
+                out=wcodes[:, j, :].bitcast(FP8X4),
+                scales=wscales[:, j, :],
+                in_=wgrp[(b, layer)][:].rearrange("p c t -> p (c t)"),
+            )
+
+        regroup_w(0, 0, None)
+
+        b0T = ps_t.tile([P, PACK, P], BF16, name="b0T", tag="t")
+        for t in range(PACK):
+            nc.tensor.transpose(b0T[:, t, :], b0rows[:, P * t : P * (t + 1)], ident_b[:])
+        b0_sb = const.tile([P, PACK, NB], F32, name="b0_sb")
+        nc.vector.tensor_copy(out=b0_sb[:], in_=b0T[:, :, 0:NB])
+        quant_w(0, 0)
+        b1_bc = const.tile([P, NB, D], F32, name="b1_bc")
+        for b in range(NB):
+            bp = ps_o.tile([P, D], F32, name="bp", tag="o")
+            nc.tensor.matmul(bp[:], lhsT=ones[:], rhs=b1row[:, D * b : D * (b + 1)], start=True, stop=True)
+            nc.scalar.copy(out=b1_bc[:, b, :], in_=bp[:])
+
+        st = {}
+
+        def transposes(i):
+            for half in range(2):
+                xt = ps_t.tile([P, 2, 2, P], F32, name="xt", tag="t")
+                for a2 in range(2):
+                    words = xraw[i][:, 2 * half + a2, :].bitcast(F32)
+                    for u in range(2):
+                        nc.tensor.transpose(xt[:, a2, u, :], words[:, P * u : P * (u + 1)], ident_f[:])
+                st[("xt", i, half)] = xt
+
+        def copy_x(i):
+            xgrp = xq.tile([P, CHUNK * PACK], BF16, name="xgrp", tag="xgrp", align_bytes=64)
+            xw = xgrp[:].bitcast(F32).rearrange("p (a r u) -> p a r u", a=TILES, r=P, u=2)
+            for half in range(2):
+                nc.scalar.copy(
+                    out=xw[:, 2 * half : 2 * half + 2, :, :],
+                    in_=st[("xt", i, half)][:].rearrange("p a u r -> p a r u"),
+                )
+            st[("xgrp", i)] = xgrp
+
+        def quant_x(i):
+            xcodes = xq.tile([P, CHUNK], U32, name="xcodes", tag="xcodes", align_bytes=64)
+            xscales = xq.tile([P, CHUNK], U8, name="xscales", tag="xscales", align_bytes=64)
+            nc.vector.quantize_mx(out=xcodes[:].bitcast(FP8X4), scales=xscales[:], in_=st[("xgrp", i)][:])
+            st[("xc", i)] = (xcodes, xscales)
+
+        def layer1(i):
+            b = i // NCH
+            xcodes, xscales = st[("xc", i)]
+            hT = hstage.tile([P, PACK, CHUNK], BF16, name="hT", tag="hT")
+            for t in range(PACK):
+                hp = ps_h.tile([P, CHUNK], F32, name="hp", tag="h")
+                nc.tensor.matmul_mx(
+                    out=hp[:],
+                    lhsT=wcodes[:, 2 * b, P * t : P * (t + 1)].bitcast(FP8X4),
+                    lhsT_scale=wscales[:, 2 * b, P * t : P * (t + 1)],
+                    rhs=xcodes[:].bitcast(FP8X4),
+                    rhs_scale=xscales[:],
+                    start=True,
+                    stop=True,
+                )
+                nc.scalar.activation(
+                    out=hT[:, t, :], in_=hp[:], func=ACT.Relu, bias=b0_sb[:, t, b : b + 1], scale=1.0
+                )
+            st[("hT", i)] = hT
+
+        def regroup_h(i):
+            hgrp = hq.tile([P, CHUNK, PACK], BF16, name="hgrp", tag="hgrp", align_bytes=64)
+            nc.vector.tensor_copy(
+                out=hgrp[:].rearrange("p (c i) t -> p c t i", i=4),
+                in_=st[("hT", i)][:].rearrange("p t (c i) -> p c t i", i=4),
+            )
+            st[("hgrp", i)] = hgrp
+
+        def quant_h(i):
+            hcodes = hq.tile([P, CHUNK], U32, name="hcodes", tag="hcodes", align_bytes=64)
+            hscales = hq.tile([P, CHUNK], U8, name="hscales", tag="hscales", align_bytes=64)
+            nc.vector.quantize_mx(
+                out=hcodes[:].bitcast(FP8X4),
+                scales=hscales[:],
+                in_=st[("hgrp", i)][:].rearrange("p c t -> p (c t)"),
+            )
+            st[("hc", i)] = (hcodes, hscales)
+
+        def layer2(i):
+            b = i // NCH
+            hcodes, hscales = st[("hc", i)]
+            osb = ostage.tile([P, TILES, D], F32, name="osb", tag="osb")
+            for a in range(TILES):
+                op = ps_o.tile([P, D], F32, name="op", tag="o")
+                nc.tensor.matmul_mx(
+                    out=op[:],
+                    lhsT=hcodes[:, P * a : P * (a + 1)].bitcast(FP8X4),
+                    lhsT_scale=hscales[:, P * a : P * (a + 1)],
+                    rhs=wcodes[:, 2 * b + 1, :].bitcast(FP8X4),
+                    rhs_scale=wscales[:, 2 * b + 1, :],
+                    start=True,
+                    stop=True,
+                )
+                nc.vector.tensor_tensor(out=osb[:, a, :], in0=op[:], in1=b1_bc[:, b, :], op=ALU.add)
+            st[("osb", i)] = osb
+
+        def relu_store(i):
+            b, c = divmod(i, NCH)
+            osb = st[("osb", i)]
+            dst = out[b].rearrange("(m a) e -> m a e", a=APP)
+            for half in range(2):
+                rows = slice(2 * half, 2 * half + 2)
+                nc.gpsimd.tensor_scalar(
+                    out=osb[:, rows, :],
+                    in0=osb[:, rows, :],
+                    scalar1=FLT_MAX,
+                    scalar2=0.0,
+                    op0=ALU.min,
+                    op1=ALU.max,
+                )
+                nc.sync.dma_start(
+                    out=dst[:, TILES * c + 2 * half : TILES * c + 2 * half + 2, :], in_=osb[:, rows, :]
+                )
+
+        transposes(0)
+        for j in range(TOTAL + 5):
+            if j < TOTAL:
+                copy_x(j)
+            if 0 <= j - 3 < TOTAL:
+                quant_h(j - 3)
+            if 0 <= j - 1 < TOTAL:
+                layer1(j - 1)
+            if 0 <= j - 2 < TOTAL:
+                regroup_h(j - 2)
+            if 0 <= j - 3 < TOTAL:
+                layer2(j - 3)
+            if 0 <= j - 4 < TOTAL:
+                relu_store(j - 4)
+            if 4 <= j < TOTAL - 4:
+                load_x(j + 4)
+                if j % NCH == 0:
+                    load_w(j // NCH + 1, 0)
+                    load_w(j // NCH + 1, 1)
+            if j < TOTAL:
+                quant_x(j)
+            if j + 1 < TOTAL:
+                transposes(j + 1)
+            if j == 0:
+                regroup_w(0, 1, None)
+            if j == 1:
+                quant_w(0, 1)
+            b, c = divmod(j - 2, NCH)
+            if 0 <= b and b + 1 < NB:
+                regroup_w(b + 1, c // 2, c % 2)
+            b, c = divmod(j - 4, NCH)
+            if 0 <= b and b + 1 < NB and c % 2 == 0:
+                quant_w(b + 1, c // 2)

@@ -11,7 +11,7 @@ FP8X4 = mybir.dt.float8_e4m3fn_x4
 ACT = mybir.ActivationFunctionType
 ALU = mybir.AluOpType
 
-PINNED = False
+PINNED = True
 
 P = 128
 NB = 4

@@ -12,6 +12,10 @@ ACT = mybir.ActivationFunctionType
 ALU = mybir.AluOpType
 
 PINNED = True
+RELU_A = "G"
+RELU_B = "G"
+HR = "S"
+HR_PARTS = 2
 
 P = 128
 NB = 4
@@ -43,24 +47,8 @@ def tile_can_t_kernel(tc, user_emb, item_emb, out):
         hq = ctx.enter_context(tc.tile_pool(name="hq", bufs=2))
         ostage = ctx.enter_context(tc.tile_pool(name="ostage", bufs=4))
         ps_t = ctx.enter_context(tc.psum_pool(name="ps_t", bufs=2))
-        ps_h = ctx.enter_context(tc.psum_pool(name="ps_h", bufs=4))
-        ps_o = ctx.enter_context(tc.psum_pool(name="ps_o", bufs=2))
-
-        ones = const.tile([P, P], BF16, name="ones")
-        nc.vector.memset(ones[:], 1.0)
-        b0rows = const.tile([P, D], BF16, name="b0rows")
-        nc.vector.memset(b0rows[:], 0.0)
-        b1row = const.tile([P, NB * D], BF16, name="b1row")
-        nc.vector.memset(b1row[:], 0.0)
-        nc.scalar.dma_start(out=b0rows[0:NB, :], in_=item_emb[:, OFF_B0 : OFF_B0 + D])
-        nc.scalar.dma_start(
-            out=b1row[0:1, :].rearrange("o (b e) -> o b e", b=NB),
-            in_=item_emb[:, OFF_B1 : OFF_B1 + D].unsqueeze(0),
-        )
-        ident_f = const.tile([P, P], F32, name="ident_f")
-        make_identity(nc, ident_f[:])
-        ident_b = const.tile([P, P], BF16, name="ident_b")
-        make_identity(nc, ident_b[:])
+        ps_h = ctx.enter_context(tc.psum_pool(name="ps_h", bufs=3))
+        ps_o = ctx.enter_context(tc.psum_pool(name="ps_o", bufs=3))
 
         wraw = {}
         xraw = {}
@@ -84,8 +72,20 @@ def tile_can_t_kernel(tc, user_emb, item_emb, out):
             nc.sync.dma_start(out=t[:], in_=src[:, TILES * c : TILES * (c + 1), :])
             xraw[i] = t
 
+        b0rows = const.tile([P, D], BF16, name="b0rows")
+        nc.vector.memset(b0rows[:], 0.0)
+        b1row = const.tile([P, NB * D], BF16, name="b1row")
+        nc.vector.memset(b1row[:], 0.0)
+        ones = const.tile([P, P], BF16, name="ones")
+        nc.vector.memset(ones[:], 1.0)
+
         load_w(0, 0)
         load_x(0)
+        nc.sync.dma_start(out=b0rows[0:NB, :], in_=item_emb[:, OFF_B0 : OFF_B0 + D])
+        nc.sync.dma_start(
+            out=b1row[0:1, :].rearrange("o (b e) -> o b e", b=NB),
+            in_=item_emb[:, OFF_B1 : OFF_B1 + D].unsqueeze(0),
+        )
         load_w(0, 1)
         for i in range(1, 5):
             load_x(i)
@@ -94,10 +94,15 @@ def tile_can_t_kernel(tc, user_emb, item_emb, out):
         for i in range(5, 8):
             load_x(i)
 
+        ident_f = const.tile([P, P], F32, name="ident_f")
+        make_identity(nc, ident_f[:])
+        ident_b = const.tile([P, P], BF16, name="ident_b")
+        make_identity(nc, ident_b[:])
+
         wcodes = const.tile([P, 2 * NB, D], U32, name="wcodes", align_bytes=64)
         wscales = const.tile([P, 2 * NB, D], U8, name="wscales", align_bytes=64)
         wgrp = {}
-        HALF = D // 4 // 2
+        PIECE = D // 4 // HR_PARTS
 
         def regroup_w(b, layer, part):
             if part is None or part == 0:
@@ -106,9 +111,19 @@ def tile_can_t_kernel(tc, user_emb, item_emb, out):
             src = wraw[(b, layer)][:].rearrange("p t (c i) -> p c t i", i=4)
             if part is None:
                 nc.vector.tensor_copy(out=dst, in_=src)
-            else:
-                cols = slice(HALF * part, HALF * (part + 1))
+                return
+            cols = slice(PIECE * part, PIECE * (part + 1))
+            if HR == "S":
                 nc.scalar.copy(out=dst[:, cols, :, :], in_=src[:, cols, :, :])
+            else:
+                nc.gpsimd.tensor_scalar(
+                    out=dst[:, cols, :, :],
+                    in0=src[:, cols, :, :],
+                    scalar1=1.0,
+                    scalar2=0.0,
+                    op0=ALU.mult,
+                    op1=ALU.add,
+                )
 
         def quant_w(b, layer):
             j = 2 * b + layer
@@ -118,40 +133,24 @@ def tile_can_t_kernel(tc, user_emb, item_emb, out):
                 in_=wgrp[(b, layer)][:].rearrange("p c t -> p (c t)"),
             )
 
-        regroup_w(0, 0, None)
-
-        b0T = ps_t.tile([P, PACK, P], BF16, name="b0T", tag="t")
-        for t in range(PACK):
-            nc.tensor.transpose(b0T[:, t, :], b0rows[:, P * t : P * (t + 1)], ident_b[:])
-        b0_sb = const.tile([P, PACK, NB], F32, name="b0_sb")
-        nc.vector.tensor_copy(out=b0_sb[:], in_=b0T[:, :, 0:NB])
-        quant_w(0, 0)
-        b1_bc = const.tile([P, NB, D], F32, name="b1_bc")
-        for b in range(NB):
-            bp = ps_o.tile([P, D], F32, name="bp", tag="o")
-            nc.tensor.matmul(bp[:], lhsT=ones[:], rhs=b1row[:, D * b : D * (b + 1)], start=True, stop=True)
-            nc.scalar.copy(out=b1_bc[:, b, :], in_=bp[:])
-
         st = {}
 
-        def transposes(i):
-            for half in range(2):
-                xt = ps_t.tile([P, 2, 2, P], F32, name="xt", tag="t")
-                for a2 in range(2):
-                    words = xraw[i][:, 2 * half + a2, :].bitcast(F32)
-                    for u in range(2):
-                        nc.tensor.transpose(xt[:, a2, u, :], words[:, P * u : P * (u + 1)], ident_f[:])
-                st[("xt", i, half)] = xt
+        def transposes(i, half):
+            xt = ps_t.tile([P, 2, 2, P], F32, name="xt", tag="t")
+            for a2 in range(2):
+                words = xraw[i][:, 2 * half + a2, :].bitcast(F32)
+                for u in range(2):
+                    nc.tensor.transpose(xt[:, a2, u, :], words[:, P * u : P * (u + 1)], ident_f[:])
+            st[("xt", i, half)] = xt
 
-        def copy_x(i):
-            xgrp = xq.tile([P, CHUNK * PACK], BF16, name="xgrp", tag="xgrp", align_bytes=64)
-            xw = xgrp[:].bitcast(F32).rearrange("p (a r u) -> p a r u", a=TILES, r=P, u=2)
-            for half in range(2):
-                nc.scalar.copy(
-                    out=xw[:, 2 * half : 2 * half + 2, :, :],
-                    in_=st[("xt", i, half)][:].rearrange("p a u r -> p a r u"),
-                )
-            st[("xgrp", i)] = xgrp
+        def copy_x(i, half):
+            if half == 0:
+                st[("xgrp", i)] = xq.tile([P, CHUNK * PACK], BF16, name="xgrp", tag="xgrp", align_bytes=64)
+            xw = st[("xgrp", i)][:].bitcast(F32).rearrange("p (a r u) -> p a r u", a=TILES, r=P, u=2)
+            nc.scalar.copy(
+                out=xw[:, 2 * half : 2 * half + 2, :, :],
+                in_=st[("xt", i, half)][:].rearrange("p a u r -> p a r u"),
+            )
 
         def quant_x(i):
             xcodes = xq.tile([P, CHUNK], U32, name="xcodes", tag="xcodes", align_bytes=64)
@@ -159,25 +158,32 @@ def tile_can_t_kernel(tc, user_emb, item_emb, out):
             nc.vector.quantize_mx(out=xcodes[:].bitcast(FP8X4), scales=xscales[:], in_=st[("xgrp", i)][:])
             st[("xc", i)] = (xcodes, xscales)
 
-        def layer1(i):
+        def layer1(i, t):
             b = i // NCH
             xcodes, xscales = st[("xc", i)]
-            hT = hstage.tile([P, PACK, CHUNK], BF16, name="hT", tag="hT")
-            for t in range(PACK):
-                hp = ps_h.tile([P, CHUNK], F32, name="hp", tag="h")
-                nc.tensor.matmul_mx(
-                    out=hp[:],
-                    lhsT=wcodes[:, 2 * b, P * t : P * (t + 1)].bitcast(FP8X4),
-                    lhsT_scale=wscales[:, 2 * b, P * t : P * (t + 1)],
-                    rhs=xcodes[:].bitcast(FP8X4),
-                    rhs_scale=xscales[:],
-                    start=True,
-                    stop=True,
-                )
-                nc.scalar.activation(
-                    out=hT[:, t, :], in_=hp[:], func=ACT.Relu, bias=b0_sb[:, t, b : b + 1], scale=1.0
-                )
-            st[("hT", i)] = hT
+            hp = ps_h.tile([P, CHUNK], F32, name="hp", tag="h")
+            nc.tensor.matmul_mx(
+                out=hp[:],
+                lhsT=wcodes[:, 2 * b, P * t : P * (t + 1)].bitcast(FP8X4),
+                lhsT_scale=wscales[:, 2 * b, P * t : P * (t + 1)],
+                rhs=xcodes[:].bitcast(FP8X4),
+                rhs_scale=xscales[:],
+                start=True,
+                stop=True,
+            )
+            st[("hp", i, t)] = hp
+
+        def act(i, t):
+            b = i // NCH
+            if t == 0:
+                st[("hT", i)] = hstage.tile([P, PACK, CHUNK], BF16, name="hT", tag="hT")
+            nc.scalar.activation(
+                out=st[("hT", i)][:, t, :],
+                in_=st[("hp", i, t)][:],
+                func=ACT.Relu,
+                bias=b0_sb[:, t, b : b + 1],
+                scale=1.0,
+            )
 
         def regroup_h(i):
             hgrp = hq.tile([P, CHUNK, PACK], BF16, name="hgrp", tag="hgrp", align_bytes=64)
@@ -197,72 +203,139 @@ def tile_can_t_kernel(tc, user_emb, item_emb, out):
             )
             st[("hc", i)] = (hcodes, hscales)
 
-        def layer2(i):
+        def layer2(i, a):
             b = i // NCH
             hcodes, hscales = st[("hc", i)]
-            osb = ostage.tile([P, TILES, D], F32, name="osb", tag="osb")
-            for a in range(TILES):
-                op = ps_o.tile([P, D], F32, name="op", tag="o")
-                nc.tensor.matmul_mx(
-                    out=op[:],
-                    lhsT=hcodes[:, P * a : P * (a + 1)].bitcast(FP8X4),
-                    lhsT_scale=hscales[:, P * a : P * (a + 1)],
-                    rhs=wcodes[:, 2 * b + 1, :].bitcast(FP8X4),
-                    rhs_scale=wscales[:, 2 * b + 1, :],
-                    start=True,
-                    stop=True,
-                )
-                nc.vector.tensor_tensor(out=osb[:, a, :], in0=op[:], in1=b1_bc[:, b, :], op=ALU.add)
-            st[("osb", i)] = osb
+            op = ps_o.tile([P, D], F32, name="op", tag="o")
+            nc.tensor.matmul_mx(
+                out=op[:],
+                lhsT=hcodes[:, P * a : P * (a + 1)].bitcast(FP8X4),
+                lhsT_scale=hscales[:, P * a : P * (a + 1)],
+                rhs=wcodes[:, 2 * b + 1, :].bitcast(FP8X4),
+                rhs_scale=wscales[:, 2 * b + 1, :],
+                start=True,
+                stop=True,
+            )
+            st[("op", i, a)] = op
 
-        def relu_store(i):
-            b, c = divmod(i, NCH)
-            osb = st[("osb", i)]
-            dst = out[b].rearrange("(m a) e -> m a e", a=APP)
-            for half in range(2):
-                rows = slice(2 * half, 2 * half + 2)
+        def add(i, a):
+            b = i // NCH
+            if a == 0:
+                st[("osb", i)] = ostage.tile([P, TILES, D], F32, name="osb", tag="osb")
+            nc.vector.tensor_tensor(
+                out=st[("osb", i)][:, a, :], in0=st[("op", i, a)][:], in1=b1_bc[:, b, :], op=ALU.add
+            )
+
+        def relu(i, engine, a0, a1):
+            part = st[("osb", i)][:, a0:a1, :]
+            if engine == "S":
+                nc.scalar.activation(out=part, in_=part, func=ACT.Relu)
+            elif engine == "V":
+                nc.vector.tensor_scalar_max(out=part, in0=part, scalar1=0.0)
+            else:
                 nc.gpsimd.tensor_scalar(
-                    out=osb[:, rows, :],
-                    in0=osb[:, rows, :],
-                    scalar1=FLT_MAX,
-                    scalar2=0.0,
-                    op0=ALU.min,
-                    op1=ALU.max,
-                )
-                nc.sync.dma_start(
-                    out=dst[:, TILES * c + 2 * half : TILES * c + 2 * half + 2, :], in_=osb[:, rows, :]
+                    out=part, in0=part, scalar1=FLT_MAX, scalar2=0.0, op0=ALU.min, op1=ALU.max
                 )
 
-        transposes(0)
+        def relu_store(i, half):
+            b, c = divmod(i, NCH)
+            plan = RELU_A if half == 0 else RELU_B
+            if len(plan) == 1:
+                relu(i, plan, 2 * half, 2 * half + 2)
+            else:
+                relu(i, plan[0], 2 * half, 2 * half + 1)
+                relu(i, plan[1], 2 * half + 1, 2 * half + 2)
+            dst = out[b].rearrange("(m a) e -> m a e", a=APP)
+            nc.sync.dma_start(
+                out=dst[:, TILES * c + 2 * half : TILES * c + 2 * half + 2, :],
+                in_=st[("osb", i)][:, 2 * half : 2 * half + 2, :],
+            )
+
+        regroup_w(0, 0, None)
+        transposes(0, 0)
+        transposes(0, 1)
+        b0T = ps_h.tile([P, PACK, P], BF16, name="b0T", tag="h")
+        for t in range(PACK):
+            nc.tensor.transpose(b0T[:, t, :], b0rows[:, P * t : P * (t + 1)], ident_b[:])
+        b0_sb = const.tile([P, PACK, NB], F32, name="b0_sb")
+        nc.vector.tensor_copy(out=b0_sb[:], in_=b0T[:, :, 0:NB])
+        quant_w(0, 0)
+        b1_bc = const.tile([P, NB, D], F32, name="b1_bc")
+
+        def spread_b1(b):
+            bp = ps_o.tile([P, D], F32, name="bp", tag="o")
+            nc.tensor.matmul(bp[:], lhsT=ones[:], rhs=b1row[:, D * b : D * (b + 1)], start=True, stop=True)
+            nc.vector.tensor_copy(out=b1_bc[:, b, :], in_=bp[:])
+
+        def ok(i):
+            return 0 <= i < TOTAL
+
         for j in range(TOTAL + 5):
-            if j < TOTAL:
-                copy_x(j)
-            if 0 <= j - 3 < TOTAL:
-                quant_h(j - 3)
-            if 0 <= j - 1 < TOTAL:
-                layer1(j - 1)
-            if 0 <= j - 2 < TOTAL:
+            if ok(j - 3):
+                add(j - 3, 0)
+            if ok(j):
+                copy_x(j, 0)
+            if ok(j - 3):
+                layer2(j - 3, 3)
+            if ok(j - 1):
+                act(j - 1, 0)
+            if ok(j + 1):
+                transposes(j + 1, 0)
+            if ok(j - 1):
+                layer1(j - 1, 3)
+            if ok(j - 2):
                 regroup_h(j - 2)
-            if 0 <= j - 3 < TOTAL:
-                layer2(j - 3)
-            if 0 <= j - 4 < TOTAL:
-                relu_store(j - 4)
+            if ok(j):
+                copy_x(j, 1)
+            if ok(j + 1):
+                transposes(j + 1, 1)
+            if ok(j - 3):
+                add(j - 3, 1)
+            if ok(j - 1):
+                act(j - 1, 1)
+            if ok(j - 2):
+                quant_h(j - 2)
+            if ok(j - 4):
+                relu_store(j - 4, 0)
+            if ok(j - 3):
+                add(j - 3, 2)
+            if ok(j - 2):
+                layer2(j - 2, 0)
+                layer2(j - 2, 1)
+            if ok(j - 1):
+                act(j - 1, 2)
+            if ok(j):
+                quant_x(j)
+            if ok(j - 4):
+                relu_store(j - 4, 1)
+            if ok(j - 3):
+                add(j - 3, 3)
+            if ok(j):
+                layer1(j, 0)
+                layer1(j, 1)
+            if ok(j - 2):
+                layer2(j - 2, 2)
+            if ok(j - 1):
+                act(j - 1, 3)
+            if ok(j):
+                layer1(j, 2)
             if 4 <= j < TOTAL - 4:
                 load_x(j + 4)
                 if j % NCH == 0:
                     load_w(j // NCH + 1, 0)
                     load_w(j // NCH + 1, 1)
-            if j < TOTAL:
-                quant_x(j)
-            if j + 1 < TOTAL:
-                transposes(j + 1)
             if j == 0:
                 regroup_w(0, 1, None)
+                spread_b1(0)
+                spread_b1(1)
             if j == 1:
                 quant_w(0, 1)
-            b, c = divmod(j - 2, NCH)
+                spread_b1(2)
+                spread_b1(3)
+            b, c = divmod(j - 1, NCH)
             if 0 <= b and b + 1 < NB:
-                regroup_w(b + 1, c // 2, c % 2)
-            b, c = divmod(j - 4, NCH)
+                for part in range(HR_PARTS // 2):
+                    regroup_w(b + 1, c // 2, (c % 2) * (HR_PARTS // 2) + part)
+            b, c = divmod(j - 3, NCH)
             if 0 <= b and b + 1 < NB and c % 2 == 0:
                 quant_w(b + 1, c // 2)

@@ -12,10 +12,10 @@ ACT = mybir.ActivationFunctionType
 ALU = mybir.AluOpType
 
 PINNED = True
-RELU_A = "G"
-RELU_B = "G"
-HR = "S"
-HR_PARTS = 2
+RELU_A = "S"
+RELU_B = "SV"
+HR = "G"
+HR_PARTS = 4
 
 P = 128
 NB = 4

@@ -13,7 +13,7 @@ ALU = mybir.AluOpType
 
 PINNED = True
 RELU_A = "S"
-RELU_B = "SV"
+RELU_B = "S"
 HR = "G"
 HR_PARTS = 4
 

from contextlib import ExitStack

import concourse.mybir as mybir
from concourse.masks import make_identity

F32 = mybir.dt.float32
BF16 = mybir.dt.bfloat16
U32 = mybir.dt.uint32
U8 = mybir.dt.uint8
FP8X4 = mybir.dt.float8_e4m3fn_x4
ACT = mybir.ActivationFunctionType
ALU = mybir.AluOpType

PINNED = True
RELU_A = "S"
RELU_B = "S"
HR = "G"
HR_PARTS = 4

P = 128
NB = 4
NTOK = 2048
D = 512
PACK = 4
TILES = 4
CHUNK = TILES * P
NCH = NTOK // CHUNK
APP = NTOK // P
TOTAL = NB * NCH
OFF_W = (0, D * D + D)
OFF_B0 = D * D
OFF_B1 = 2 * D * D + D
FLT_MAX = 3.4028234663852886e38

FLOPS = 2 * NB * NTOK * D * D * 2


def tile_can_t_kernel(tc, user_emb, item_emb, out):
    nc = tc.nc
    with ExitStack() as ctx:
        if PINNED:
            ctx.enter_context(tc.manual_schedule())
        const = ctx.enter_context(tc.tile_pool(name="const", bufs=1))
        wstage = ctx.enter_context(tc.tile_pool(name="wstage", bufs=2))
        xq = ctx.enter_context(tc.tile_pool(name="xq", bufs=2))
        hstage = ctx.enter_context(tc.tile_pool(name="hstage", bufs=2))
        hq = ctx.enter_context(tc.tile_pool(name="hq", bufs=2))
        ostage = ctx.enter_context(tc.tile_pool(name="ostage", bufs=4))
        ps_t = ctx.enter_context(tc.psum_pool(name="ps_t", bufs=2))
        ps_h = ctx.enter_context(tc.psum_pool(name="ps_h", bufs=3))
        ps_o = ctx.enter_context(tc.psum_pool(name="ps_o", bufs=3))

        wraw = {}
        xraw = {}

        def load_w(b, layer):
            t = const.tile([P, PACK, D], BF16, name="wraw%d%d" % (b, layer))
            flat = item_emb[b, OFF_W[layer] : OFF_W[layer] + D * D]
            if layer == 0:
                nc.sync.dma_start(
                    out=t[:].rearrange("p (u e) c -> p u (e c)", u=2),
                    in_=flat.rearrange("(u p f) -> p u f", u=2, p=P, f=2 * D),
                )
            else:
                nc.sync.dma_start(out=t[:], in_=flat.rearrange("(t p c) -> p t c", t=PACK, p=P, c=D))
            wraw[(b, layer)] = t

        def load_x(i):
            b, c = divmod(i, NCH)
            t = const.tile([P, TILES, D], BF16, name="xraw%d" % i)
            src = user_emb[b].rearrange("(p a) k -> p a k", a=APP)
            nc.sync.dma_start(out=t[:], in_=src[:, TILES * c : TILES * (c + 1), :])
            xraw[i] = t

        b0rows = const.tile([P, D], BF16, name="b0rows")
        nc.vector.memset(b0rows[:], 0.0)
        b1row = const.tile([P, NB * D], BF16, name="b1row")
        nc.vector.memset(b1row[:], 0.0)
        ones = const.tile([P, P], BF16, name="ones")
        nc.vector.memset(ones[:], 1.0)

        load_w(0, 0)
        load_x(0)
        nc.sync.dma_start(out=b0rows[0:NB, :], in_=item_emb[:, OFF_B0 : OFF_B0 + D])
        nc.sync.dma_start(
            out=b1row[0:1, :].rearrange("o (b e) -> o b e", b=NB),
            in_=item_emb[:, OFF_B1 : OFF_B1 + D].unsqueeze(0),
        )
        load_w(0, 1)
        for i in range(1, 5):
            load_x(i)
        load_w(1, 0)
        load_w(1, 1)
        for i in range(5, 8):
            load_x(i)

        ident_f = const.tile([P, P], F32, name="ident_f")
        make_identity(nc, ident_f[:])
        ident_b = const.tile([P, P], BF16, name="ident_b")
        make_identity(nc, ident_b[:])

        wcodes = const.tile([P, 2 * NB, D], U32, name="wcodes", align_bytes=64)
        wscales = const.tile([P, 2 * NB, D], U8, name="wscales", align_bytes=64)
        wgrp = {}
        PIECE = D // 4 // HR_PARTS

        def regroup_w(b, layer, part):
            if part is None or part == 0:
                wgrp[(b, layer)] = wstage.tile([P, D, PACK], BF16, name="wgrp", tag="wgrp", align_bytes=64)
            dst = wgrp[(b, layer)][:].rearrange("p (c i) t -> p c t i", i=4)
            src = wraw[(b, layer)][:].rearrange("p t (c i) -> p c t i", i=4)
            if part is None:
                nc.vector.tensor_copy(out=dst, in_=src)
                return
            cols = slice(PIECE * part, PIECE * (part + 1))
            if HR == "S":
                nc.scalar.copy(out=dst[:, cols, :, :], in_=src[:, cols, :, :])
            else:
                nc.gpsimd.tensor_scalar(
                    out=dst[:, cols, :, :],
                    in0=src[:, cols, :, :],
                    scalar1=1.0,
                    scalar2=0.0,
                    op0=ALU.mult,
                    op1=ALU.add,
                )

        def quant_w(b, layer):
            j = 2 * b + layer
            nc.vector.quantize_mx(
                out=wcodes[:, j, :].bitcast(FP8X4),
                scales=wscales[:, j, :],
                in_=wgrp[(b, layer)][:].rearrange("p c t -> p (c t)"),
            )

        st = {}

        def transposes(i, half):
            xt = ps_t.tile([P, 2, 2, P], F32, name="xt", tag="t")
            for a2 in range(2):
                words = xraw[i][:, 2 * half + a2, :].bitcast(F32)
                for u in range(2):
                    nc.tensor.transpose(xt[:, a2, u, :], words[:, P * u : P * (u + 1)], ident_f[:])
            st[("xt", i, half)] = xt

        def copy_x(i, half):
            if half == 0:
                st[("xgrp", i)] = xq.tile([P, CHUNK * PACK], BF16, name="xgrp", tag="xgrp", align_bytes=64)
            xw = st[("xgrp", i)][:].bitcast(F32).rearrange("p (a r u) -> p a r u", a=TILES, r=P, u=2)
            nc.scalar.copy(
                out=xw[:, 2 * half : 2 * half + 2, :, :],
                in_=st[("xt", i, half)][:].rearrange("p a u r -> p a r u"),
            )

        def quant_x(i):
            xcodes = xq.tile([P, CHUNK], U32, name="xcodes", tag="xcodes", align_bytes=64)
            xscales = xq.tile([P, CHUNK], U8, name="xscales", tag="xscales", align_bytes=64)
            nc.vector.quantize_mx(out=xcodes[:].bitcast(FP8X4), scales=xscales[:], in_=st[("xgrp", i)][:])
            st[("xc", i)] = (xcodes, xscales)

        def layer1(i, t):
            b = i // NCH
            xcodes, xscales = st[("xc", i)]
            hp = ps_h.tile([P, CHUNK], F32, name="hp", tag="h")
            nc.tensor.matmul_mx(
                out=hp[:],
                lhsT=wcodes[:, 2 * b, P * t : P * (t + 1)].bitcast(FP8X4),
                lhsT_scale=wscales[:, 2 * b, P * t : P * (t + 1)],
                rhs=xcodes[:].bitcast(FP8X4),
                rhs_scale=xscales[:],
                start=True,
                stop=True,
            )
            st[("hp", i, t)] = hp

        def act(i, t):
            b = i // NCH
            if t == 0:
                st[("hT", i)] = hstage.tile([P, PACK, CHUNK], BF16, name="hT", tag="hT")
            nc.scalar.activation(
                out=st[("hT", i)][:, t, :],
                in_=st[("hp", i, t)][:],
                func=ACT.Relu,
                bias=b0_sb[:, t, b : b + 1],
                scale=1.0,
            )

        def regroup_h(i):
            hgrp = hq.tile([P, CHUNK, PACK], BF16, name="hgrp", tag="hgrp", align_bytes=64)
            nc.vector.tensor_copy(
                out=hgrp[:].rearrange("p (c i) t -> p c t i", i=4),
                in_=st[("hT", i)][:].rearrange("p t (c i) -> p c t i", i=4),
            )
            st[("hgrp", i)] = hgrp

        def quant_h(i):
            hcodes = hq.tile([P, CHUNK], U32, name="hcodes", tag="hcodes", align_bytes=64)
            hscales = hq.tile([P, CHUNK], U8, name="hscales", tag="hscales", align_bytes=64)
            nc.vector.quantize_mx(
                out=hcodes[:].bitcast(FP8X4),
                scales=hscales[:],
                in_=st[("hgrp", i)][:].rearrange("p c t -> p (c t)"),
            )
            st[("hc", i)] = (hcodes, hscales)

        def layer2(i, a):
            b = i // NCH
            hcodes, hscales = st[("hc", i)]
            op = ps_o.tile([P, D], F32, name="op", tag="o")
            nc.tensor.matmul_mx(
                out=op[:],
                lhsT=hcodes[:, P * a : P * (a + 1)].bitcast(FP8X4),
                lhsT_scale=hscales[:, P * a : P * (a + 1)],
                rhs=wcodes[:, 2 * b + 1, :].bitcast(FP8X4),
                rhs_scale=wscales[:, 2 * b + 1, :],
                start=True,
                stop=True,
            )
            st[("op", i, a)] = op

        def add(i, a):
            b = i // NCH
            if a == 0:
                st[("osb", i)] = ostage.tile([P, TILES, D], F32, name="osb", tag="osb")
            nc.vector.tensor_tensor(
                out=st[("osb", i)][:, a, :], in0=st[("op", i, a)][:], in1=b1_bc[:, b, :], op=ALU.add
            )

        def relu(i, engine, a0, a1):
            part = st[("osb", i)][:, a0:a1, :]
            if engine == "S":
                nc.scalar.activation(out=part, in_=part, func=ACT.Relu)
            elif engine == "V":
                nc.vector.tensor_scalar_max(out=part, in0=part, scalar1=0.0)
            else:
                nc.gpsimd.tensor_scalar(
                    out=part, in0=part, scalar1=FLT_MAX, scalar2=0.0, op0=ALU.min, op1=ALU.max
                )

        def relu_store(i, half):
            b, c = divmod(i, NCH)
            plan = RELU_A if half == 0 else RELU_B
            if len(plan) == 1:
                relu(i, plan, 2 * half, 2 * half + 2)
            else:
                relu(i, plan[0], 2 * half, 2 * half + 1)
                relu(i, plan[1], 2 * half + 1, 2 * half + 2)
            dst = out[b].rearrange("(m a) e -> m a e", a=APP)
            nc.sync.dma_start(
                out=dst[:, TILES * c + 2 * half : TILES * c + 2 * half + 2, :],
                in_=st[("osb", i)][:, 2 * half : 2 * half + 2, :],
            )

        regroup_w(0, 0, None)
        transposes(0, 0)
        transposes(0, 1)
        b0T = ps_h.tile([P, PACK, P], BF16, name="b0T", tag="h")
        for t in range(PACK):
            nc.tensor.transpose(b0T[:, t, :], b0rows[:, P * t : P * (t + 1)], ident_b[:])
        b0_sb = const.tile([P, PACK, NB], F32, name="b0_sb")
        nc.vector.tensor_copy(out=b0_sb[:], in_=b0T[:, :, 0:NB])
        quant_w(0, 0)
        b1_bc = const.tile([P, NB, D], F32, name="b1_bc")

        def spread_b1(b):
            bp = ps_o.tile([P, D], F32, name="bp", tag="o")
            nc.tensor.matmul(bp[:], lhsT=ones[:], rhs=b1row[:, D * b : D * (b + 1)], start=True, stop=True)
            nc.vector.tensor_copy(out=b1_bc[:, b, :], in_=bp[:])

        def ok(i):
            return 0 <= i < TOTAL

        for j in range(TOTAL + 5):
            if ok(j - 3):
                add(j - 3, 0)
            if ok(j):
                copy_x(j, 0)
            if ok(j - 3):
                layer2(j - 3, 3)
            if ok(j - 1):
                act(j - 1, 0)
            if ok(j + 1):
                transposes(j + 1, 0)
            if ok(j - 1):
                layer1(j - 1, 3)
            if ok(j - 2):
                regroup_h(j - 2)
            if ok(j):
                copy_x(j, 1)
            if ok(j + 1):
                transposes(j + 1, 1)
            if ok(j - 3):
                add(j - 3, 1)
            if ok(j - 1):
                act(j - 1, 1)
            if ok(j - 2):
                quant_h(j - 2)
            if ok(j - 4):
                relu_store(j - 4, 0)
            if ok(j - 3):
                add(j - 3, 2)
            if ok(j - 2):
                layer2(j - 2, 0)
                layer2(j - 2, 1)
            if ok(j - 1):
                act(j - 1, 2)
            if ok(j):
                quant_x(j)
            if ok(j - 4):
                relu_store(j - 4, 1)
            if ok(j - 3):
                add(j - 3, 3)
            if ok(j):
                layer1(j, 0)
                layer1(j, 1)
            if ok(j - 2):
                layer2(j - 2, 2)
            if ok(j - 1):
                act(j - 1, 3)
            if ok(j):
                layer1(j, 2)
            if 4 <= j < TOTAL - 4:
                load_x(j + 4)
                if j % NCH == 0:
                    load_w(j // NCH + 1, 0)
                    load_w(j // NCH + 1, 1)
            if j == 0:
                regroup_w(0, 1, None)
                spread_b1(0)
                spread_b1(1)
            if j == 1:
                quant_w(0, 1)
                spread_b1(2)
                spread_b1(3)
            b, c = divmod(j - 1, NCH)
            if 0 <= b and b + 1 < NB:
                for part in range(HR_PARTS // 2):
                    regroup_w(b + 1, c // 2, (c % 2) * (HR_PARTS // 2) + part)
            b, c = divmod(j - 3, NCH)
            if 0 <= b and b + 1 < NB and c % 2 == 0:
                quant_w(b + 1, c // 2)
